import numpy as np
import ml_dtypes


def mxq(x, axis, fmt="e4m3"):
    dtype, down = {"e4m3": (ml_dtypes.float8_e4m3fn, 7), "e5m2": (ml_dtypes.float8_e5m2, 14)}[fmt]
    v = np.moveaxis(np.asarray(x, np.float32).astype(ml_dtypes.bfloat16).astype(np.float64), axis, -1)
    blocks = v.reshape(v.shape[:-1] + (-1, 32))
    amax = np.abs(blocks).max(-1, keepdims=True)
    byte = np.maximum(np.where(amax > 0, np.frexp(amax)[1] - 1 + 127, 0) - down, 1)
    scale = np.exp2(byte - 127.0)
    codes = (blocks / scale).astype(np.float32).astype(dtype).astype(np.float64)
    return np.moveaxis((codes * scale).reshape(v.shape), -1, axis)


WIDE = False


def mx_kscale(k):
    if not WIDE:
        return np.ones(k)
    levels = np.array([10, -10, 5, -5, 0])
    a = np.random.permutation(np.resize(levels, k // 512 * 4)).reshape(k // 512, 4)
    idx = np.arange(k)
    return np.exp2(a[idx // 512, idx % 128 // 32])


BF16 = ml_dtypes.bfloat16


def bf(x):
    return np.asarray(x, np.float32).astype(BF16)


def f64(x):
    return np.asarray(x).astype(np.float64)


B, N, D, F = 4, 32, 512, 512


def setup_inputs():
    s, t = mx_kscale(D), mx_kscale(D)
    ss = np.concatenate([s, s])
    sst = np.concatenate([s, s, t])
    return {
        'text_embedding': bf(np.random.standard_normal((B, N, D)) * s),
        'W_rel': bf(np.random.standard_normal((2 * D, D)) / np.sqrt(2 * D) / ss[:, None] * t),
        'b_rel': bf(np.random.standard_normal(D) * 0.3 * t),
        'W_go': bf(np.random.standard_normal((D, D)) / np.sqrt(D) / s[:, None]),
        'b_go': bf(np.random.standard_normal(D) * 0.3),
        'W_gr': bf(np.random.standard_normal((3 * D, F)) * 1.5 / np.sqrt(3 * D) / sst[:, None]),
        'b_gr': bf(np.random.standard_normal(F) * 0.3),
    }


def reference(text_embedding, W_rel, b_rel, W_go, b_go, W_gr, b_gr):
    xq = mxq(f64(text_embedding), 2, 'e4m3')
    wr, wg = f64(W_rel), f64(W_gr)
    new_x = np.tanh((xq @ mxq(f64(W_go), 0, 'e4m3')) + f64(b_go))
    rel0 = ((xq @ mxq(wr[:D], 0, 'e4m3'))[:, :, None, :]
            + (xq @ mxq(wr[D:], 0, 'e4m3'))[:, None, :, :] + f64(b_rel))
    pre = ((xq @ mxq(wg[:D], 0, 'e4m3'))[:, :, None, :]
           + (xq @ mxq(wg[D:2 * D], 0, 'e4m3'))[:, None, :, :]
           + (mxq(rel0, 3, 'e4m3') @ mxq(wg[2 * D:], 0, 'e4m3')) + f64(b_gr))
    return new_x, np.tanh(pre)

@@ -1,0 +1,249 @@
+from contextlib import ExitStack
+
+import concourse.mybir as mybir
+from concourse.masks import make_identity
+
+BF16 = mybir.dt.bfloat16
+F32 = mybir.dt.float32
+I32 = mybir.dt.int32
+U32 = mybir.dt.uint32
+U8 = mybir.dt.uint8
+FP8X4 = mybir.dt.float8_e4m3fn_x4
+ADD = mybir.AluOpType.add
+TANH = mybir.ActivationFunctionType.Tanh
+
+P = 128
+PACK = 4
+BATCH = 4
+NODES = 32
+TOKENS = BATCH * NODES
+D = P * PACK
+F = 512
+PAIRS = BATCH * NODES * NODES
+I_PER_TILE = P // NODES
+I_PER_CHUNK = 16
+COLS_PER_CHUNK = I_PER_CHUNK * NODES
+TILES_PER_CHUNK = COLS_PER_CHUNK // P
+CHUNKS = PAIRS // COLS_PER_CHUNK
+BYTES_PER_WORD = 4
+
+FLOPS = 2 * (5 * TOKENS * D * F + PAIRS * D * F)
+
+
+def load_weight(nc, pool, rows, name):
+    raw = pool.tile([P, PACK, F], BF16, name=name)
+    nc.sync.dma_start(out=raw[:], in_=rows.rearrange("(t p) n -> p t n", p=P))
+    return raw
+
+
+def quantise_weight(nc, pool, copy, raw, name):
+    grouped = pool.tile([P, F, PACK], BF16, name=name + "_grouped", align_bytes=64)
+    copy(
+        out=grouped[:].rearrange("p (c i) t -> p c t i", i=4),
+        in_=raw[:].rearrange("p t (c i) -> p c t i", i=4),
+    )
+    codes = pool.tile([P, F], U32, name=name + "_codes", align_bytes=64)
+    scales = pool.tile([P, F], U8, name=name + "_scales", align_bytes=64)
+    nc.vector.quantize_mx(
+        out=codes[:].bitcast(FP8X4), scales=scales[:], in_=grouped[:].rearrange("p n t -> p (n t)")
+    )
+    return codes, scales
+
+
+def columns(operand, first, count):
+    codes, scales = operand
+    return codes[:, first : first + count], scales[:, first : first + count]
+
+
+def mx_pass(nc, out, stationary, moving, start, stop):
+    nc.tensor.matmul_mx(
+        out=out,
+        lhsT=stationary[0].bitcast(FP8X4),
+        lhsT_scale=stationary[1],
+        rhs=moving[0].bitcast(FP8X4),
+        rhs_scale=moving[1],
+        start=start,
+        stop=stop,
+    )
+
+
+def tile_languagemsgencoder_pa_kernel(
+    tc, text_embedding, W_rel, b_rel, W_go, b_go, W_gr, b_gr, out_0, out_1
+):
+    nc = tc.nc
+    new_x_rows = out_0.rearrange("b n f -> (b n) f")
+    rel_rows = out_1.rearrange("b i j f -> (b i j) f")
+
+    with ExitStack() as ctx:
+        keep = ctx.enter_context(tc.tile_pool(name="keep", bufs=1))
+        stream = ctx.enter_context(tc.tile_pool(name="stream", bufs=3))
+        results = ctx.enter_context(tc.tile_pool(name="results", bufs=6))
+        keep_ps = ctx.enter_context(tc.psum_pool(name="keep_ps", bufs=1))
+        setup_ps = ctx.enter_context(tc.psum_pool(name="setup_ps", bufs=3))
+        acc_ps = ctx.enter_context(tc.psum_pool(name="acc_ps", bufs=4))
+
+        x_sb = keep.tile([P, D], BF16)
+        nc.sync.dma_start(out=x_sb[:], in_=text_embedding.rearrange("b n d -> (b n) d"))
+        ra_raw = load_weight(nc, keep, W_rel[0:D, :], "ra_raw")
+        rb_raw = load_weight(nc, keep, W_rel[D : 2 * D, :], "rb_raw")
+        gc_raw = load_weight(nc, keep, W_gr[2 * D : 3 * D, :], "gc_raw")
+        ga_raw = load_weight(nc, keep, W_gr[0:D, :], "ga_raw")
+        gb_raw = load_weight(nc, keep, W_gr[D : 2 * D, :], "gb_raw")
+        go_raw = load_weight(nc, keep, W_go, "go_raw")
+
+        brel_rows = keep.tile([P, P], BF16)
+        nc.vector.memset(brel_rows[:], 0.0)
+        nc.scalar.dma_start(out=brel_rows[0:PACK, :], in_=b_rel.rearrange("(t m) -> t m", m=P))
+        bias_rows = keep.tile([P, 2, F], BF16)
+        nc.vector.memset(bias_rows[:], 0.0)
+        nc.scalar.dma_start(out=bias_rows[0:1, 0, :], in_=b_gr.rearrange("(o f) -> o f", o=1))
+        nc.scalar.dma_start(out=bias_rows[0:1, 1, :], in_=b_go.rearrange("(o f) -> o f", o=1))
+
+        warm = keep.tile([P, 1], F32)
+        nc.vector.memset(warm[:], 0.0)
+        nc.scalar.activation(out=warm[:], in_=warm[:], func=TANH)
+
+        ident = keep.tile([P, P], BF16)
+        make_identity(nc, ident[:])
+        ones = keep.tile([P, P], BF16)
+        nc.vector.memset(ones[:], 1.0)
+
+        x_t = setup_ps.tile([P, PACK, TOKENS], BF16, tag="setup")
+        for t in range(PACK):
+            nc.tensor.transpose(x_t[:, t, :], x_sb[:, t * P : (t + 1) * P], ident[:])
+        x_grouped = keep.tile([P, TOKENS, PACK], BF16, align_bytes=64)
+        nc.scalar.copy(out=x_grouped[:], in_=x_t[:].rearrange("p t r -> p r t"))
+        x_fourfold = keep.tile([P, TOKENS, BYTES_PER_WORD, PACK], BF16, align_bytes=64)
+        nc.vector.tensor_copy(
+            out=x_fourfold[:],
+            in_=x_grouped[:].unsqueeze(2).to_broadcast([P, TOKENS, BYTES_PER_WORD, PACK]),
+        )
+
+        x_codes = keep.tile([P, TOKENS], U32, align_bytes=64)
+        x_scales = keep.tile([P, TOKENS], U8, align_bytes=64)
+        x4_codes = keep.tile([P, TOKENS * BYTES_PER_WORD], U32, align_bytes=64)
+        x4_scales = keep.tile([P, TOKENS * BYTES_PER_WORD], U8, align_bytes=64)
+        nc.vector.memset(x_scales[:].bitcast(I32), 0)
+        nc.vector.memset(x4_scales[:].bitcast(I32), 0)
+        nc.vector.quantize_mx(
+            out=x_codes[:].bitcast(FP8X4), scales=x_scales[:], in_=x_grouped[:].rearrange("p r t -> p (r t)")
+        )
+        nc.vector.quantize_mx(
+            out=x4_codes[:].bitcast(FP8X4),
+            scales=x4_scales[:],
+            in_=x_fourfold[:].rearrange("p r c t -> p (r c t)"),
+        )
+        x_mx = (x_codes[:], x_scales[:])
+
+        brel_t = setup_ps.tile([P, P], BF16, tag="setup")
+        nc.tensor.transpose(brel_t[:], brel_rows[:], ident[:])
+        brel = keep.tile([P, PACK], F32)
+        nc.vector.tensor_copy(out=brel[:], in_=brel_t[:, 0:PACK])
+
+        spread = []
+        for v in range(2):
+            bias_ps = setup_ps.tile([P, F], F32, tag="setup")
+            nc.tensor.matmul(out=bias_ps[:], lhsT=ones[:], rhs=bias_rows[:, v, :], start=True, stop=True)
+            bias_sb = keep.tile([P, F], F32, name="bias_sb%d" % v)
+            nc.scalar.copy(out=bias_sb[:], in_=bias_ps[:])
+            spread.append(bias_sb)
+        bgr, bgo = spread
+
+        ra = quantise_weight(nc, keep, nc.vector.tensor_copy, ra_raw, "ra")
+        rb = quantise_weight(nc, keep, nc.vector.tensor_copy, rb_raw, "rb")
+        a_t = setup_ps.tile([P, PACK, TOKENS], F32, tag="setup")
+        b_t = keep_ps.tile([P, PACK, TOKENS], F32)
+        for t in range(PACK):
+            mx_pass(nc, a_t[:, t, :], columns(ra, t * P, P), x_mx, start=True, stop=True)
+        for t in range(PACK):
+            mx_pass(nc, b_t[:, t, :], columns(rb, t * P, P), x_mx, start=True, stop=True)
+        a_plus = keep.tile([P, TOKENS, PACK], F32)
+        nc.vector.tensor_tensor(
+            out=a_plus[:],
+            in0=a_t[:].rearrange("p t r -> p r t"),
+            in1=brel[:].unsqueeze(1).to_broadcast([P, TOKENS, PACK]),
+            op=ADD,
+        )
+
+        xj_codes = keep.tile([P, TOKENS * I_PER_TILE], U32, align_bytes=64)
+        xj_scales = keep.tile([P, TOKENS * I_PER_TILE], U8, align_bytes=64)
+        nc.vector.tensor_copy(
+            out=xj_codes[:].bitcast(I32).rearrange("p (b c j) -> p b c j", b=BATCH, c=I_PER_TILE),
+            in_=x_codes[:]
+            .bitcast(I32)
+            .rearrange("p (b j) -> p b j", b=BATCH)
+            .unsqueeze(2)
+            .to_broadcast([P, BATCH, I_PER_TILE, NODES]),
+        )
+        nc.vector.tensor_copy(
+            out=xj_scales[:].bitcast(I32).rearrange("p (b c w) -> p b c w", b=BATCH, c=I_PER_TILE),
+            in_=x_scales[:]
+            .bitcast(I32)
+            .rearrange("p (b w) -> p b w", b=BATCH)
+            .unsqueeze(2)
+            .to_broadcast([P, BATCH, I_PER_TILE, NODES // BYTES_PER_WORD]),
+        )
+        xj = (xj_codes, xj_scales)
+        xi_codes = keep.tile([P, PAIRS], U32, align_bytes=64)
+        xi_scales = keep.tile([P, PAIRS], U8, align_bytes=64)
+        repeats = NODES // BYTES_PER_WORD
+        for b in range(BATCH):
+            tokens = slice(b * NODES, (b + 1) * NODES)
+            nc.vector.tensor_copy(
+                out=xi_codes[:]
+                .bitcast(I32)
+                .rearrange("p (r e c) -> p r e c", e=repeats, c=BYTES_PER_WORD)[:, tokens, :, :],
+                in_=x4_codes[:]
+                .bitcast(I32)
+                .rearrange("p (r c) -> p r c", c=BYTES_PER_WORD)[:, tokens, :]
+                .unsqueeze(2)
+                .to_broadcast([P, NODES, repeats, BYTES_PER_WORD]),
+            )
+            nc.vector.tensor_copy(
+                out=xi_scales[:].bitcast(I32).rearrange("p (r e) -> p r e", e=repeats)[:, tokens, :],
+                in_=x4_scales[:].bitcast(I32)[:, tokens].unsqueeze(2).to_broadcast([P, NODES, repeats]),
+            )
+        xi = (xi_codes, xi_scales)
+
+        gc = quantise_weight(nc, keep, nc.scalar.copy, gc_raw, "gc")
+        ga = quantise_weight(nc, keep, nc.scalar.copy, ga_raw, "ga")
+        gb = quantise_weight(nc, keep, nc.scalar.copy, gb_raw, "gb")
+
+        def finish(acc, bias, rows):
+            result = results.tile([P, F], F32)
+            nc.vector.tensor_tensor(out=result[:], in0=acc[:], in1=bias[:], op=ADD)
+            nc.scalar.activation(out=result[:], in_=result[:], func=TANH)
+            nc.sync.dma_start(out=rows, in_=result[:])
+
+        rel0_codes = keep.tile([P, PAIRS], U32, align_bytes=64)
+        rel0_scales = keep.tile([P, PAIRS], U8, align_bytes=64)
+        rel0_mx = (rel0_codes, rel0_scales)
+        for chunk in range(CHUNKS):
+            first_col = chunk * COLS_PER_CHUNK
+            first_token = first_col // NODES
+            b = first_token // NODES
+            shape = [P, I_PER_CHUNK, NODES, PACK]
+            rel0 = stream.tile(shape, BF16, align_bytes=64)
+            nc.vector.tensor_tensor(
+                out=rel0[:],
+                in0=b_t[:, :, b * NODES : (b + 1) * NODES].rearrange("p t j -> p j t").unsqueeze(1).to_broadcast(shape),
+                in1=a_plus[:, first_token : first_token + I_PER_CHUNK, :].unsqueeze(2).to_broadcast(shape),
+                op=ADD,
+            )
+            chunk_codes, chunk_scales = columns(rel0_mx, first_col, COLS_PER_CHUNK)
+            nc.vector.quantize_mx(
+                out=chunk_codes.bitcast(FP8X4), scales=chunk_scales, in_=rel0[:].rearrange("p i j t -> p (i j t)")
+            )
+            for tile_in_chunk in range(TILES_PER_CHUNK):
+                first_row = first_col + tile_in_chunk * P
+                acc = acc_ps.tile([P, F], F32)
+                mx_pass(nc, acc[:], columns(xi, first_row, P), columns(ga, 0, F), start=True, stop=False)
+                mx_pass(nc, acc[:], columns(xj, b * P, P), columns(gb, 0, F), start=False, stop=False)
+                mx_pass(nc, acc[:], columns(rel0_mx, first_row, P), columns(gc, 0, F), start=False, stop=True)
+                finish(acc, bgr, rel_rows[first_row : first_row + P, :])
+
+            if chunk == 1:
+                go = quantise_weight(nc, keep, nc.scalar.copy, go_raw, "go")
+                acc = acc_ps.tile([P, F], F32)
+                mx_pass(nc, acc[:], x_mx, columns(go, 0, F), start=True, stop=True)
+                finish(acc, bgo, new_x_rows)

@@ -25,7 +25,10 @@ I_PER_CHUNK = 16
 COLS_PER_CHUNK = I_PER_CHUNK * NODES
 TILES_PER_CHUNK = COLS_PER_CHUNK // P
 CHUNKS = PAIRS // COLS_PER_CHUNK
+CHUNKS_PER_BATCH = NODES // I_PER_CHUNK
 BYTES_PER_WORD = 4
+GPSIMD_I = 10
+GPSIMD_PARTS = 2
 
 FLOPS = 2 * (5 * TOKENS * D * F + PAIRS * D * F)
 
@@ -36,12 +39,16 @@ def load_weight(nc, pool, rows, name):
     return raw
 
 
-def quantise_weight(nc, pool, copy, raw, name):
-    grouped = pool.tile([P, F, PACK], BF16, name=name + "_grouped", align_bytes=64)
+def regroup_weight(pool, copy, raw, name):
+    grouped = pool.tile([P, F, PACK], BF16, name=name, align_bytes=64)
     copy(
         out=grouped[:].rearrange("p (c i) t -> p c t i", i=4),
         in_=raw[:].rearrange("p t (c i) -> p c t i", i=4),
     )
+    return grouped
+
+
+def quantise_weight(nc, pool, grouped, name):
     codes = pool.tile([P, F], U32, name=name + "_codes", align_bytes=64)
     scales = pool.tile([P, F], U8, name=name + "_scales", align_bytes=64)
     nc.vector.quantize_mx(
@@ -76,26 +83,27 @@ def tile_languagemsgencoder_pa_kernel(
 
     with ExitStack() as ctx:
         keep = ctx.enter_context(tc.tile_pool(name="keep", bufs=1))
-        stream = ctx.enter_context(tc.tile_pool(name="stream", bufs=3))
-        results = ctx.enter_context(tc.tile_pool(name="results", bufs=6))
+        stream = ctx.enter_context(tc.tile_pool(name="stream", bufs=1))
+        results = ctx.enter_context(tc.tile_pool(name="results", bufs=8))
         keep_ps = ctx.enter_context(tc.psum_pool(name="keep_ps", bufs=1))
         setup_ps = ctx.enter_context(tc.psum_pool(name="setup_ps", bufs=3))
-        acc_ps = ctx.enter_context(tc.psum_pool(name="acc_ps", bufs=4))
+        acc_ps = ctx.enter_context(tc.psum_pool(name="acc_ps", bufs=TILES_PER_CHUNK))
+        ctx.enter_context(tc.manual_schedule())
 
         x_sb = keep.tile([P, D], BF16)
         nc.sync.dma_start(out=x_sb[:], in_=text_embedding.rearrange("b n d -> (b n) d"))
-        ra_raw = load_weight(nc, keep, W_rel[0:D, :], "ra_raw")
         rb_raw = load_weight(nc, keep, W_rel[D : 2 * D, :], "rb_raw")
-        gc_raw = load_weight(nc, keep, W_gr[2 * D : 3 * D, :], "gc_raw")
+        ra_raw = load_weight(nc, keep, W_rel[0:D, :], "ra_raw")
         ga_raw = load_weight(nc, keep, W_gr[0:D, :], "ga_raw")
         gb_raw = load_weight(nc, keep, W_gr[D : 2 * D, :], "gb_raw")
+        gc_raw = load_weight(nc, keep, W_gr[2 * D : 3 * D, :], "gc_raw")
         go_raw = load_weight(nc, keep, W_go, "go_raw")
 
         brel_rows = keep.tile([P, P], BF16)
         nc.vector.memset(brel_rows[:], 0.0)
-        nc.scalar.dma_start(out=brel_rows[0:PACK, :], in_=b_rel.rearrange("(t m) -> t m", m=P))
         bias_rows = keep.tile([P, 2, F], BF16)
         nc.vector.memset(bias_rows[:], 0.0)
+        nc.scalar.dma_start(out=brel_rows[0:PACK, :], in_=b_rel.rearrange("(t m) -> t m", m=P))
         nc.scalar.dma_start(out=bias_rows[0:1, 0, :], in_=b_gr.rearrange("(o f) -> o f", o=1))
         nc.scalar.dma_start(out=bias_rows[0:1, 1, :], in_=b_go.rearrange("(o f) -> o f", o=1))
 
@@ -108,6 +116,13 @@ def tile_languagemsgencoder_pa_kernel(
         ones = keep.tile([P, P], BF16)
         nc.vector.memset(ones[:], 1.0)
 
+        x_codes = keep.tile([P, TOKENS], U32, align_bytes=64)
+        x_scales = keep.tile([P, TOKENS], U8, align_bytes=64)
+        x4_codes = keep.tile([P, TOKENS * BYTES_PER_WORD], U32, align_bytes=64)
+        x4_scales = keep.tile([P, TOKENS * BYTES_PER_WORD], U8, align_bytes=64)
+        nc.vector.memset(x_scales[:].bitcast(I32), 0)
+        nc.vector.memset(x4_scales[:].bitcast(I32), 0)
+
         x_t = setup_ps.tile([P, PACK, TOKENS], BF16, tag="setup")
         for t in range(PACK):
             nc.tensor.transpose(x_t[:, t, :], x_sb[:, t * P : (t + 1) * P], ident[:])
@@ -118,20 +133,8 @@ def tile_languagemsgencoder_pa_kernel(
             out=x_fourfold[:],
             in_=x_grouped[:].unsqueeze(2).to_broadcast([P, TOKENS, BYTES_PER_WORD, PACK]),
         )
-
-        x_codes = keep.tile([P, TOKENS], U32, align_bytes=64)
-        x_scales = keep.tile([P, TOKENS], U8, align_bytes=64)
-        x4_codes = keep.tile([P, TOKENS * BYTES_PER_WORD], U32, align_bytes=64)
-        x4_scales = keep.tile([P, TOKENS * BYTES_PER_WORD], U8, align_bytes=64)
-        nc.vector.memset(x_scales[:].bitcast(I32), 0)
-        nc.vector.memset(x4_scales[:].bitcast(I32), 0)
         nc.vector.quantize_mx(
             out=x_codes[:].bitcast(FP8X4), scales=x_scales[:], in_=x_grouped[:].rearrange("p r t -> p (r t)")
-        )
-        nc.vector.quantize_mx(
-            out=x4_codes[:].bitcast(FP8X4),
-            scales=x4_scales[:],
-            in_=x_fourfold[:].rearrange("p r c t -> p (r c t)"),
         )
         x_mx = (x_codes[:], x_scales[:])
 
@@ -139,31 +142,14 @@ def tile_languagemsgencoder_pa_kernel(
         nc.tensor.transpose(brel_t[:], brel_rows[:], ident[:])
         brel = keep.tile([P, PACK], F32)
         nc.vector.tensor_copy(out=brel[:], in_=brel_t[:, 0:PACK])
+        bgr_ps = setup_ps.tile([P, F], F32, tag="setup")
+        nc.tensor.matmul(out=bgr_ps[:], lhsT=ones[:], rhs=bias_rows[:, 0, :], start=True, stop=True)
+        bgo_ps = setup_ps.tile([P, F], F32, tag="setup")
+        nc.tensor.matmul(out=bgo_ps[:], lhsT=ones[:], rhs=bias_rows[:, 1, :], start=True, stop=True)
 
-        spread = []
-        for v in range(2):
-            bias_ps = setup_ps.tile([P, F], F32, tag="setup")
-            nc.tensor.matmul(out=bias_ps[:], lhsT=ones[:], rhs=bias_rows[:, v, :], start=True, stop=True)
-            bias_sb = keep.tile([P, F], F32, name="bias_sb%d" % v)
-            nc.scalar.copy(out=bias_sb[:], in_=bias_ps[:])
-            spread.append(bias_sb)
-        bgr, bgo = spread
-
-        ra = quantise_weight(nc, keep, nc.vector.tensor_copy, ra_raw, "ra")
-        rb = quantise_weight(nc, keep, nc.vector.tensor_copy, rb_raw, "rb")
-        a_t = setup_ps.tile([P, PACK, TOKENS], F32, tag="setup")
-        b_t = keep_ps.tile([P, PACK, TOKENS], F32)
-        for t in range(PACK):
-            mx_pass(nc, a_t[:, t, :], columns(ra, t * P, P), x_mx, start=True, stop=True)
-        for t in range(PACK):
-            mx_pass(nc, b_t[:, t, :], columns(rb, t * P, P), x_mx, start=True, stop=True)
-        a_plus = keep.tile([P, TOKENS, PACK], F32)
-        nc.vector.tensor_tensor(
-            out=a_plus[:],
-            in0=a_t[:].rearrange("p t r -> p r t"),
-            in1=brel[:].unsqueeze(1).to_broadcast([P, TOKENS, PACK]),
-            op=ADD,
-        )
+        rb_grouped = regroup_weight(keep, nc.scalar.copy, rb_raw, "rb_grouped")
+        bgr = keep.tile([P, F], F32)
+        nc.scalar.copy(out=bgr[:], in_=bgr_ps[:])
 
         xj_codes = keep.tile([P, TOKENS * I_PER_TILE], U32, align_bytes=64)
         xj_scales = keep.tile([P, TOKENS * I_PER_TILE], U8, align_bytes=64)
@@ -184,10 +170,46 @@ def tile_languagemsgencoder_pa_kernel(
             .to_broadcast([P, BATCH, I_PER_TILE, NODES // BYTES_PER_WORD]),
         )
         xj = (xj_codes, xj_scales)
+        nc.vector.quantize_mx(
+            out=x4_codes[:].bitcast(FP8X4),
+            scales=x4_scales[:],
+            in_=x_fourfold[:].rearrange("p r c t -> p (r c t)"),
+        )
+
+        ra_grouped = regroup_weight(keep, nc.vector.tensor_copy, ra_raw, "ra_grouped")
+        rb = quantise_weight(nc, keep, rb_grouped, "rb")
+        b_t = setup_ps.tile([P, PACK, TOKENS], F32, tag="setup")
+        for t in range(PACK):
+            mx_pass(nc, b_t[:, t, :], columns(rb, t * P, P), x_mx, start=True, stop=True)
+        ra = quantise_weight(nc, keep, ra_grouped, "ra")
+        a_t = keep_ps.tile([P, PACK, TOKENS], F32)
+        a_t_copy = setup_ps.tile([P, PACK, TOKENS], F32, tag="setup")
+        for t in range(PACK):
+            mx_pass(nc, a_t_copy[:, t, :], columns(ra, t * P, P), x_mx, start=True, stop=True)
+        for t in range(PACK):
+            mx_pass(nc, a_t[:, t, :], columns(ra, t * P, P), x_mx, start=True, stop=True)
+        b_plus = keep.tile([P, TOKENS, PACK], F32)
+        nc.vector.tensor_tensor(
+            out=b_plus[:],
+            in0=b_t[:].rearrange("p t r -> p r t"),
+            in1=brel[:].unsqueeze(1).to_broadcast([P, TOKENS, PACK]),
+            op=ADD,
+        )
+        ga_grouped = regroup_weight(keep, nc.scalar.copy, ga_raw, "ga_grouped")
+        a_sb = keep.tile([P, TOKENS, PACK], F32)
+        nc.scalar.copy(out=a_sb[:], in_=a_t_copy[:].rearrange("p t r -> p r t"))
+        bgo = keep.tile([P, F], F32)
+        nc.scalar.copy(out=bgo[:], in_=bgo_ps[:])
+        gb_grouped = regroup_weight(keep, nc.scalar.copy, gb_raw, "gb_grouped")
+        gc_grouped = regroup_weight(keep, nc.scalar.copy, gc_raw, "gc_grouped")
+        go_grouped = regroup_weight(keep, nc.scalar.copy, go_raw, "go_grouped")
+
         xi_codes = keep.tile([P, PAIRS], U32, align_bytes=64)
         xi_scales = keep.tile([P, PAIRS], U8, align_bytes=64)
+        xi = (xi_codes, xi_scales)
         repeats = NODES // BYTES_PER_WORD
-        for b in range(BATCH):
+
+        def repeat_xi(b):
             tokens = slice(b * NODES, (b + 1) * NODES)
             nc.vector.tensor_copy(
                 out=xi_codes[:]
@@ -203,11 +225,53 @@ def tile_languagemsgencoder_pa_kernel(
                 out=xi_scales[:].bitcast(I32).rearrange("p (r e) -> p r e", e=repeats)[:, tokens, :],
                 in_=x4_scales[:].bitcast(I32)[:, tokens].unsqueeze(2).to_broadcast([P, NODES, repeats]),
             )
-        xi = (xi_codes, xi_scales)
 
-        gc = quantise_weight(nc, keep, nc.scalar.copy, gc_raw, "gc")
-        ga = quantise_weight(nc, keep, nc.scalar.copy, ga_raw, "ga")
-        gb = quantise_weight(nc, keep, nc.scalar.copy, gb_raw, "gb")
+        rel0_codes = keep.tile([P, PAIRS], U32, align_bytes=64)
+        rel0_scales = keep.tile([P, PAIRS], U8, align_bytes=64)
+        rel0_mx = (rel0_codes, rel0_scales)
+
+        def form_rel0(chunk):
+            first_token = chunk * I_PER_CHUNK
+            b = first_token // NODES
+            rel0 = stream.tile([P, I_PER_CHUNK, NODES, PACK], BF16, align_bytes=64)
+            b_part = b_plus[:, b * NODES : (b + 1) * NODES, :].unsqueeze(1)
+            count = GPSIMD_I // GPSIMD_PARTS
+            for first in range(0, GPSIMD_I, count):
+                nc.gpsimd.tensor_tensor(
+                    out=rel0[:, first : first + count, :, :],
+                    in0=a_sb[:, first_token + first : first_token + first + count, :]
+                    .unsqueeze(2)
+                    .to_broadcast([P, count, NODES, PACK]),
+                    in1=b_part.to_broadcast([P, count, NODES, PACK]),
+                    op=ADD,
+                )
+            count = I_PER_CHUNK - GPSIMD_I
+            nc.vector.tensor_tensor(
+                out=rel0[:, GPSIMD_I:I_PER_CHUNK, :, :],
+                in0=a_t[:, :, first_token + GPSIMD_I : first_token + I_PER_CHUNK]
+                .rearrange("p t i -> p i t")
+                .unsqueeze(2)
+                .to_broadcast([P, count, NODES, PACK]),
+                in1=b_part.to_broadcast([P, count, NODES, PACK]),
+                op=ADD,
+            )
+            return rel0
+
+        def quantise_rel0(chunk, rel0):
+            chunk_codes, chunk_scales = columns(rel0_mx, chunk * COLS_PER_CHUNK, COLS_PER_CHUNK)
+            nc.vector.quantize_mx(
+                out=chunk_codes.bitcast(FP8X4), scales=chunk_scales, in_=rel0[:].rearrange("p i j t -> p (i j t)")
+            )
+
+        def open_tile(first_row):
+            b = first_row // (NODES * NODES)
+            acc = acc_ps.tile([P, F], F32)
+            mx_pass(nc, acc[:], columns(xi, first_row, P), columns(ga, 0, F), start=True, stop=False)
+            mx_pass(nc, acc[:], columns(xj, b * P, P), columns(gb, 0, F), start=False, stop=False)
+            return acc
+
+        def close_tile(acc, first_row):
+            mx_pass(nc, acc[:], columns(rel0_mx, first_row, P), columns(gc, 0, F), start=False, stop=True)
 
         def finish(acc, bias, rows):
             result = results.tile([P, F], F32)
@@ -215,35 +279,32 @@ def tile_languagemsgencoder_pa_kernel(
             nc.scalar.activation(out=result[:], in_=result[:], func=TANH)
             nc.sync.dma_start(out=rows, in_=result[:])
 
-        rel0_codes = keep.tile([P, PAIRS], U32, align_bytes=64)
-        rel0_scales = keep.tile([P, PAIRS], U8, align_bytes=64)
-        rel0_mx = (rel0_codes, rel0_scales)
+        repeat_xi(0)
+        accs = []
         for chunk in range(CHUNKS):
-            first_col = chunk * COLS_PER_CHUNK
-            first_token = first_col // NODES
-            b = first_token // NODES
-            shape = [P, I_PER_CHUNK, NODES, PACK]
-            rel0 = stream.tile(shape, BF16, align_bytes=64)
-            nc.vector.tensor_tensor(
-                out=rel0[:],
-                in0=b_t[:, :, b * NODES : (b + 1) * NODES].rearrange("p t j -> p j t").unsqueeze(1).to_broadcast(shape),
-                in1=a_plus[:, first_token : first_token + I_PER_CHUNK, :].unsqueeze(2).to_broadcast(shape),
-                op=ADD,
-            )
-            chunk_codes, chunk_scales = columns(rel0_mx, first_col, COLS_PER_CHUNK)
-            nc.vector.quantize_mx(
-                out=chunk_codes.bitcast(FP8X4), scales=chunk_scales, in_=rel0[:].rearrange("p i j t -> p (i j t)")
-            )
-            for tile_in_chunk in range(TILES_PER_CHUNK):
-                first_row = first_col + tile_in_chunk * P
-                acc = acc_ps.tile([P, F], F32)
-                mx_pass(nc, acc[:], columns(xi, first_row, P), columns(ga, 0, F), start=True, stop=False)
-                mx_pass(nc, acc[:], columns(xj, b * P, P), columns(gb, 0, F), start=False, stop=False)
-                mx_pass(nc, acc[:], columns(rel0_mx, first_row, P), columns(gc, 0, F), start=False, stop=True)
-                finish(acc, bgr, rel_rows[first_row : first_row + P, :])
-
-            if chunk == 1:
-                go = quantise_weight(nc, keep, nc.scalar.copy, go_raw, "go")
-                acc = acc_ps.tile([P, F], F32)
-                mx_pass(nc, acc[:], x_mx, columns(go, 0, F), start=True, stop=True)
-                finish(acc, bgo, new_x_rows)
+            rel0 = form_rel0(chunk)
+            if chunk == 0:
+                ga = quantise_weight(nc, keep, ga_grouped, "ga")
+                gb = quantise_weight(nc, keep, gb_grouped, "gb")
+            opened = []
+            for n in range(TILES_PER_CHUNK):
+                first_row = chunk * COLS_PER_CHUNK + n * P
+                if chunk > 0:
+                    finish(accs[n], bgr, rel_rows[first_row - COLS_PER_CHUNK : first_row - COLS_PER_CHUNK + P, :])
+                opened.append(open_tile(first_row))
+            accs = opened
+            if chunk == 0:
+                gc = quantise_weight(nc, keep, gc_grouped, "gc")
+            if (chunk + 1) % CHUNKS_PER_BATCH == 0 and chunk + 1 < CHUNKS:
+                repeat_xi((chunk + 1) // CHUNKS_PER_BATCH)
+            if chunk == CHUNKS - 1:
+                go = quantise_weight(nc, keep, go_grouped, "go")
+                new_x_acc = setup_ps.tile([P, F], F32, tag="setup")
+                mx_pass(nc, new_x_acc[:], x_mx, columns(go, 0, F), start=True, stop=True)
+            quantise_rel0(chunk, rel0)
+            for n in range(TILES_PER_CHUNK):
+                close_tile(accs[n], chunk * COLS_PER_CHUNK + n * P)
+        finish(new_x_acc, bgo, new_x_rows)
+        for n in range(TILES_PER_CHUNK):
+            first_row = (CHUNKS - 1) * COLS_PER_CHUNK + n * P
+            finish(accs[n], bgr, rel_rows[first_row : first_row + P, :])

@@ -28,7 +28,7 @@ CHUNKS = PAIRS // COLS_PER_CHUNK
 CHUNKS_PER_BATCH = NODES // I_PER_CHUNK
 BYTES_PER_WORD = 4
 GPSIMD_I = 10
-GPSIMD_PARTS = 2
+GPSIMD_PARTS = 1
 
 FLOPS = 2 * (5 * TOKENS * D * F + PAIRS * D * F)
 
@@ -176,34 +176,6 @@ def tile_languagemsgencoder_pa_kernel(
             in_=x_fourfold[:].rearrange("p r c t -> p (r c t)"),
         )
 
-        ra_grouped = regroup_weight(keep, nc.vector.tensor_copy, ra_raw, "ra_grouped")
-        rb = quantise_weight(nc, keep, rb_grouped, "rb")
-        b_t = setup_ps.tile([P, PACK, TOKENS], F32, tag="setup")
-        for t in range(PACK):
-            mx_pass(nc, b_t[:, t, :], columns(rb, t * P, P), x_mx, start=True, stop=True)
-        ra = quantise_weight(nc, keep, ra_grouped, "ra")
-        a_t = keep_ps.tile([P, PACK, TOKENS], F32)
-        a_t_copy = setup_ps.tile([P, PACK, TOKENS], F32, tag="setup")
-        for t in range(PACK):
-            mx_pass(nc, a_t_copy[:, t, :], columns(ra, t * P, P), x_mx, start=True, stop=True)
-        for t in range(PACK):
-            mx_pass(nc, a_t[:, t, :], columns(ra, t * P, P), x_mx, start=True, stop=True)
-        b_plus = keep.tile([P, TOKENS, PACK], F32)
-        nc.vector.tensor_tensor(
-            out=b_plus[:],
-            in0=b_t[:].rearrange("p t r -> p r t"),
-            in1=brel[:].unsqueeze(1).to_broadcast([P, TOKENS, PACK]),
-            op=ADD,
-        )
-        ga_grouped = regroup_weight(keep, nc.scalar.copy, ga_raw, "ga_grouped")
-        a_sb = keep.tile([P, TOKENS, PACK], F32)
-        nc.scalar.copy(out=a_sb[:], in_=a_t_copy[:].rearrange("p t r -> p r t"))
-        bgo = keep.tile([P, F], F32)
-        nc.scalar.copy(out=bgo[:], in_=bgo_ps[:])
-        gb_grouped = regroup_weight(keep, nc.scalar.copy, gb_raw, "gb_grouped")
-        gc_grouped = regroup_weight(keep, nc.scalar.copy, gc_raw, "gc_grouped")
-        go_grouped = regroup_weight(keep, nc.scalar.copy, go_raw, "go_grouped")
-
         xi_codes = keep.tile([P, PAIRS], U32, align_bytes=64)
         xi_scales = keep.tile([P, PAIRS], U8, align_bytes=64)
         xi = (xi_codes, xi_scales)
@@ -225,6 +197,32 @@ def tile_languagemsgencoder_pa_kernel(
                 out=xi_scales[:].bitcast(I32).rearrange("p (r e) -> p r e", e=repeats)[:, tokens, :],
                 in_=x4_scales[:].bitcast(I32)[:, tokens].unsqueeze(2).to_broadcast([P, NODES, repeats]),
             )
+
+        ra_grouped = regroup_weight(keep, nc.vector.tensor_copy, ra_raw, "ra_grouped")
+        rb = quantise_weight(nc, keep, rb_grouped, "rb")
+        b_t = setup_ps.tile([P, PACK, TOKENS], F32, tag="setup")
+        for t in range(PACK):
+            mx_pass(nc, b_t[:, t, :], columns(rb, t * P, P), x_mx, start=True, stop=True)
+        ra = quantise_weight(nc, keep, ra_grouped, "ra")
+        a_t = keep_ps.tile([P, PACK, TOKENS], F32)
+        for t in range(PACK):
+            mx_pass(nc, a_t[:, t, :], columns(ra, t * P, P), x_mx, start=True, stop=True)
+        repeat_xi(0)
+        b_plus = keep.tile([P, TOKENS, PACK], F32)
+        nc.vector.tensor_tensor(
+            out=b_plus[:],
+            in0=b_t[:].rearrange("p t r -> p r t"),
+            in1=brel[:].unsqueeze(1).to_broadcast([P, TOKENS, PACK]),
+            op=ADD,
+        )
+        a_sb = keep.tile([P, TOKENS, PACK], F32)
+        nc.vector.tensor_copy(out=a_sb[:], in_=a_t[:].rearrange("p t r -> p r t"))
+        ga_grouped = regroup_weight(keep, nc.scalar.copy, ga_raw, "ga_grouped")
+        gb_grouped = regroup_weight(keep, nc.scalar.copy, gb_raw, "gb_grouped")
+        gc_grouped = regroup_weight(keep, nc.scalar.copy, gc_raw, "gc_grouped")
+        go_grouped = regroup_weight(keep, nc.scalar.copy, go_raw, "go_grouped")
+        bgo = keep.tile([P, F], F32)
+        nc.scalar.copy(out=bgo[:], in_=bgo_ps[:])
 
         rel0_codes = keep.tile([P, PAIRS], U32, align_bytes=64)
         rel0_scales = keep.tile([P, PAIRS], U8, align_bytes=64)
@@ -279,7 +277,6 @@ def tile_languagemsgencoder_pa_kernel(
             nc.scalar.activation(out=result[:], in_=result[:], func=TANH)
             nc.sync.dma_start(out=rows, in_=result[:])
 
-        repeat_xi(0)
         accs = []
         for chunk in range(CHUNKS):
             rel0 = form_rel0(chunk)

@@ -28,14 +28,16 @@ CHUNKS = PAIRS // COLS_PER_CHUNK
 CHUNKS_PER_BATCH = NODES // I_PER_CHUNK
 BYTES_PER_WORD = 4
 GPSIMD_I = 10
-GPSIMD_PARTS = 1
+
+BY_FEATURE = "(p t) n -> p t n"
+BY_CHANNEL = "(t p) n -> p t n"
 
 FLOPS = 2 * (5 * TOKENS * D * F + PAIRS * D * F)
 
 
-def load_weight(nc, pool, rows, name):
+def load_weight(nc, pool, rows, order, name):
     raw = pool.tile([P, PACK, F], BF16, name=name)
-    nc.sync.dma_start(out=raw[:], in_=rows.rearrange("(t p) n -> p t n", p=P))
+    nc.sync.dma_start(out=raw[:], in_=rows.rearrange(order, p=P))
     return raw
 
 
@@ -92,12 +94,12 @@ def tile_languagemsgencoder_pa_kernel(
 
         x_sb = keep.tile([P, D], BF16)
         nc.sync.dma_start(out=x_sb[:], in_=text_embedding.rearrange("b n d -> (b n) d"))
-        rb_raw = load_weight(nc, keep, W_rel[D : 2 * D, :], "rb_raw")
-        ra_raw = load_weight(nc, keep, W_rel[0:D, :], "ra_raw")
-        ga_raw = load_weight(nc, keep, W_gr[0:D, :], "ga_raw")
-        gb_raw = load_weight(nc, keep, W_gr[D : 2 * D, :], "gb_raw")
-        gc_raw = load_weight(nc, keep, W_gr[2 * D : 3 * D, :], "gc_raw")
-        go_raw = load_weight(nc, keep, W_go, "go_raw")
+        rb_raw = load_weight(nc, keep, W_rel[D : 2 * D, :], BY_FEATURE, "rb_raw")
+        ra_raw = load_weight(nc, keep, W_rel[0:D, :], BY_FEATURE, "ra_raw")
+        ga_raw = load_weight(nc, keep, W_gr[0:D, :], BY_FEATURE, "ga_raw")
+        gb_raw = load_weight(nc, keep, W_gr[D : 2 * D, :], BY_FEATURE, "gb_raw")
+        gc_raw = load_weight(nc, keep, W_gr[2 * D : 3 * D, :], BY_CHANNEL, "gc_raw")
+        go_raw = load_weight(nc, keep, W_go, BY_FEATURE, "go_raw")
 
         brel_rows = keep.tile([P, P], BF16)
         nc.vector.memset(brel_rows[:], 0.0)
@@ -111,7 +113,7 @@ def tile_languagemsgencoder_pa_kernel(
         nc.vector.memset(warm[:], 0.0)
         nc.scalar.activation(out=warm[:], in_=warm[:], func=TANH)
 
-        ident = keep.tile([P, P], BF16)
+        ident = keep.tile([P, P], F32)
         make_identity(nc, ident[:])
         ones = keep.tile([P, P], BF16)
         nc.vector.memset(ones[:], 1.0)
@@ -123,11 +125,15 @@ def tile_languagemsgencoder_pa_kernel(
         nc.vector.memset(x_scales[:].bitcast(I32), 0)
         nc.vector.memset(x4_scales[:].bitcast(I32), 0)
 
-        x_t = setup_ps.tile([P, PACK, TOKENS], BF16, tag="setup")
-        for t in range(PACK):
-            nc.tensor.transpose(x_t[:, t, :], x_sb[:, t * P : (t + 1) * P], ident[:])
+        x_words = x_sb[:].bitcast(F32)
+        x_t = setup_ps.tile([P, 2, TOKENS], F32, tag="setup")
+        for u in range(2):
+            nc.tensor.transpose(x_t[:, u, :], x_words[:, u : D // 2 : 2], ident[:])
         x_grouped = keep.tile([P, TOKENS, PACK], BF16, align_bytes=64)
-        nc.scalar.copy(out=x_grouped[:], in_=x_t[:].rearrange("p t r -> p r t"))
+        nc.scalar.copy(
+            out=x_grouped[:].rearrange("p r t -> p (r t)").bitcast(F32).rearrange("p (r u) -> p r u", u=2),
+            in_=x_t[:].rearrange("p u r -> p r u"),
+        )
         x_fourfold = keep.tile([P, TOKENS, BYTES_PER_WORD, PACK], BF16, align_bytes=64)
         nc.vector.tensor_copy(
             out=x_fourfold[:],
@@ -138,18 +144,16 @@ def tile_languagemsgencoder_pa_kernel(
         )
         x_mx = (x_codes[:], x_scales[:])
 
-        brel_t = setup_ps.tile([P, P], BF16, tag="setup")
-        nc.tensor.transpose(brel_t[:], brel_rows[:], ident[:])
-        brel = keep.tile([P, PACK], F32)
-        nc.vector.tensor_copy(out=brel[:], in_=brel_t[:, 0:PACK])
+        brel_rows_f32 = keep.tile([P, P], F32)
+        nc.vector.tensor_copy(out=brel_rows_f32[:], in_=brel_rows[:])
+        brel_t = setup_ps.tile([P, P], F32, tag="setup")
+        nc.tensor.transpose(brel_t[:], brel_rows_f32[:], ident[:])
         bgr_ps = setup_ps.tile([P, F], F32, tag="setup")
         nc.tensor.matmul(out=bgr_ps[:], lhsT=ones[:], rhs=bias_rows[:, 0, :], start=True, stop=True)
         bgo_ps = setup_ps.tile([P, F], F32, tag="setup")
         nc.tensor.matmul(out=bgo_ps[:], lhsT=ones[:], rhs=bias_rows[:, 1, :], start=True, stop=True)
 
         rb_grouped = regroup_weight(keep, nc.scalar.copy, rb_raw, "rb_grouped")
-        bgr = keep.tile([P, F], F32)
-        nc.scalar.copy(out=bgr[:], in_=bgr_ps[:])
 
         xj_codes = keep.tile([P, TOKENS * I_PER_TILE], U32, align_bytes=64)
         xj_scales = keep.tile([P, TOKENS * I_PER_TILE], U8, align_bytes=64)
@@ -175,6 +179,8 @@ def tile_languagemsgencoder_pa_kernel(
             scales=x4_scales[:],
             in_=x_fourfold[:].rearrange("p r c t -> p (r c t)"),
         )
+        brel = keep.tile([P, PACK], F32)
+        nc.vector.tensor_copy(out=brel[:], in_=brel_t[:, 0:PACK])
 
         xi_codes = keep.tile([P, PAIRS], U32, align_bytes=64)
         xi_scales = keep.tile([P, PAIRS], U8, align_bytes=64)
@@ -220,6 +226,8 @@ def tile_languagemsgencoder_pa_kernel(
         ga_grouped = regroup_weight(keep, nc.scalar.copy, ga_raw, "ga_grouped")
         gb_grouped = regroup_weight(keep, nc.scalar.copy, gb_raw, "gb_grouped")
         gc_grouped = regroup_weight(keep, nc.scalar.copy, gc_raw, "gc_grouped")
+        bgr = keep.tile([P, F], F32)
+        nc.scalar.copy(out=bgr[:], in_=bgr_ps[:])
         go_grouped = regroup_weight(keep, nc.scalar.copy, go_raw, "go_grouped")
         bgo = keep.tile([P, F], F32)
         nc.scalar.copy(out=bgo[:], in_=bgo_ps[:])
@@ -228,29 +236,27 @@ def tile_languagemsgencoder_pa_kernel(
         rel0_scales = keep.tile([P, PAIRS], U8, align_bytes=64)
         rel0_mx = (rel0_codes, rel0_scales)
 
-        def form_rel0(chunk):
+        def form_rel0(chunk, gpsimd_i):
             first_token = chunk * I_PER_CHUNK
             b = first_token // NODES
             rel0 = stream.tile([P, I_PER_CHUNK, NODES, PACK], BF16, align_bytes=64)
             b_part = b_plus[:, b * NODES : (b + 1) * NODES, :].unsqueeze(1)
-            count = GPSIMD_I // GPSIMD_PARTS
-            for first in range(0, GPSIMD_I, count):
-                nc.gpsimd.tensor_tensor(
-                    out=rel0[:, first : first + count, :, :],
-                    in0=a_sb[:, first_token + first : first_token + first + count, :]
-                    .unsqueeze(2)
-                    .to_broadcast([P, count, NODES, PACK]),
-                    in1=b_part.to_broadcast([P, count, NODES, PACK]),
-                    op=ADD,
-                )
-            count = I_PER_CHUNK - GPSIMD_I
+            nc.gpsimd.tensor_tensor(
+                out=rel0[:, 0:gpsimd_i, :, :],
+                in0=a_sb[:, first_token : first_token + gpsimd_i, :]
+                .unsqueeze(2)
+                .to_broadcast([P, gpsimd_i, NODES, PACK]),
+                in1=b_part.to_broadcast([P, gpsimd_i, NODES, PACK]),
+                op=ADD,
+            )
+            vector_i = I_PER_CHUNK - gpsimd_i
             nc.vector.tensor_tensor(
-                out=rel0[:, GPSIMD_I:I_PER_CHUNK, :, :],
-                in0=a_t[:, :, first_token + GPSIMD_I : first_token + I_PER_CHUNK]
+                out=rel0[:, gpsimd_i:I_PER_CHUNK, :, :],
+                in0=a_t[:, :, first_token + gpsimd_i : first_token + I_PER_CHUNK]
                 .rearrange("p t i -> p i t")
                 .unsqueeze(2)
-                .to_broadcast([P, count, NODES, PACK]),
-                in1=b_part.to_broadcast([P, count, NODES, PACK]),
+                .to_broadcast([P, vector_i, NODES, PACK]),
+                in1=b_part.to_broadcast([P, vector_i, NODES, PACK]),
                 op=ADD,
             )
             return rel0
@@ -277,31 +283,35 @@ def tile_languagemsgencoder_pa_kernel(
             nc.scalar.activation(out=result[:], in_=result[:], func=TANH)
             nc.sync.dma_start(out=rows, in_=result[:])
 
-        accs = []
-        for chunk in range(CHUNKS):
-            rel0 = form_rel0(chunk)
-            if chunk == 0:
-                ga = quantise_weight(nc, keep, ga_grouped, "ga")
-                gb = quantise_weight(nc, keep, gb_grouped, "gb")
-            opened = []
+        def first_row_of(chunk, n):
+            return chunk * COLS_PER_CHUNK + n * P
+
+        def finish_rel(chunk, n, acc):
+            finish(acc, bgr, rel_rows[first_row_of(chunk, n) : first_row_of(chunk, n) + P, :])
+
+        rel0 = form_rel0(0, I_PER_CHUNK - GPSIMD_I)
+        ga = quantise_weight(nc, keep, ga_grouped, "ga")
+        gb = quantise_weight(nc, keep, gb_grouped, "gb")
+        accs = [open_tile(first_row_of(0, n)) for n in range(TILES_PER_CHUNK)]
+        gc = quantise_weight(nc, keep, gc_grouped, "gc")
+        quantise_rel0(0, rel0)
+        for n in range(TILES_PER_CHUNK):
+            close_tile(accs[n], first_row_of(0, n))
+
+        for chunk in range(1, CHUNKS):
+            rel0 = form_rel0(chunk, GPSIMD_I)
             for n in range(TILES_PER_CHUNK):
-                first_row = chunk * COLS_PER_CHUNK + n * P
-                if chunk > 0:
-                    finish(accs[n], bgr, rel_rows[first_row - COLS_PER_CHUNK : first_row - COLS_PER_CHUNK + P, :])
-                opened.append(open_tile(first_row))
-            accs = opened
-            if chunk == 0:
-                gc = quantise_weight(nc, keep, gc_grouped, "gc")
+                finish_rel(chunk - 1, n, accs[n])
+                accs[n] = open_tile(first_row_of(chunk, n))
             if (chunk + 1) % CHUNKS_PER_BATCH == 0 and chunk + 1 < CHUNKS:
                 repeat_xi((chunk + 1) // CHUNKS_PER_BATCH)
-            if chunk == CHUNKS - 1:
-                go = quantise_weight(nc, keep, go_grouped, "go")
-                new_x_acc = setup_ps.tile([P, F], F32, tag="setup")
-                mx_pass(nc, new_x_acc[:], x_mx, columns(go, 0, F), start=True, stop=True)
             quantise_rel0(chunk, rel0)
             for n in range(TILES_PER_CHUNK):
-                close_tile(accs[n], chunk * COLS_PER_CHUNK + n * P)
-        finish(new_x_acc, bgo, new_x_rows)
+                close_tile(accs[n], first_row_of(chunk, n))
+
+        go = quantise_weight(nc, keep, go_grouped, "go")
+        new_x_acc = setup_ps.tile([P, F], F32, tag="setup")
+        mx_pass(nc, new_x_acc[:], x_mx, columns(go, 0, F), start=True, stop=True)
         for n in range(TILES_PER_CHUNK):
-            first_row = (CHUNKS - 1) * COLS_PER_CHUNK + n * P
-            finish(accs[n], bgr, rel_rows[first_row : first_row + P, :])
+            finish_rel(CHUNKS - 1, n, accs[n])
+        finish(new_x_acc, bgo, new_x_rows)

from contextlib import ExitStack

import concourse.mybir as mybir
from concourse.masks import make_identity

BF16 = mybir.dt.bfloat16
F32 = mybir.dt.float32
I32 = mybir.dt.int32
U32 = mybir.dt.uint32
U8 = mybir.dt.uint8
FP8X4 = mybir.dt.float8_e4m3fn_x4
ADD = mybir.AluOpType.add
TANH = mybir.ActivationFunctionType.Tanh

P = 128
PACK = 4
BATCH = 4
NODES = 32
TOKENS = BATCH * NODES
D = P * PACK
F = 512
PAIRS = BATCH * NODES * NODES
I_PER_TILE = P // NODES
I_PER_CHUNK = 16
COLS_PER_CHUNK = I_PER_CHUNK * NODES
TILES_PER_CHUNK = COLS_PER_CHUNK // P
CHUNKS = PAIRS // COLS_PER_CHUNK
CHUNKS_PER_BATCH = NODES // I_PER_CHUNK
BYTES_PER_WORD = 4
GPSIMD_I = 10

BY_FEATURE = "(p t) n -> p t n"
BY_CHANNEL = "(t p) n -> p t n"

FLOPS = 2 * (5 * TOKENS * D * F + PAIRS * D * F)


def load_weight(nc, pool, rows, order, name):
    raw = pool.tile([P, PACK, F], BF16, name=name)
    nc.sync.dma_start(out=raw[:], in_=rows.rearrange(order, p=P))
    return raw


def regroup_weight(pool, copy, raw, name):
    grouped = pool.tile([P, F, PACK], BF16, name=name, align_bytes=64)
    copy(
        out=grouped[:].rearrange("p (c i) t -> p c t i", i=4),
        in_=raw[:].rearrange("p t (c i) -> p c t i", i=4),
    )
    return grouped


def quantise_weight(nc, pool, grouped, name):
    codes = pool.tile([P, F], U32, name=name + "_codes", align_bytes=64)
    scales = pool.tile([P, F], U8, name=name + "_scales", align_bytes=64)
    nc.vector.quantize_mx(
        out=codes[:].bitcast(FP8X4), scales=scales[:], in_=grouped[:].rearrange("p n t -> p (n t)")
    )
    return codes, scales


def columns(operand, first, count):
    codes, scales = operand
    return codes[:, first : first + count], scales[:, first : first + count]


def mx_pass(nc, out, stationary, moving, start, stop):
    nc.tensor.matmul_mx(
        out=out,
        lhsT=stationary[0].bitcast(FP8X4),
        lhsT_scale=stationary[1],
        rhs=moving[0].bitcast(FP8X4),
        rhs_scale=moving[1],
        start=start,
        stop=stop,
    )


def tile_languagemsgencoder_pa_kernel(
    tc, text_embedding, W_rel, b_rel, W_go, b_go, W_gr, b_gr, out_0, out_1
):
    nc = tc.nc
    new_x_rows = out_0.rearrange("b n f -> (b n) f")
    rel_rows = out_1.rearrange("b i j f -> (b i j) f")

    with ExitStack() as ctx:
        keep = ctx.enter_context(tc.tile_pool(name="keep", bufs=1))
        stream = ctx.enter_context(tc.tile_pool(name="stream", bufs=1))
        results = ctx.enter_context(tc.tile_pool(name="results", bufs=8))
        keep_ps = ctx.enter_context(tc.psum_pool(name="keep_ps", bufs=1))
        setup_ps = ctx.enter_context(tc.psum_pool(name="setup_ps", bufs=3))
        acc_ps = ctx.enter_context(tc.psum_pool(name="acc_ps", bufs=TILES_PER_CHUNK))
        ctx.enter_context(tc.manual_schedule())

        x_sb = keep.tile([P, D], BF16)
        nc.sync.dma_start(out=x_sb[:], in_=text_embedding.rearrange("b n d -> (b n) d"))
        rb_raw = load_weight(nc, keep, W_rel[D : 2 * D, :], BY_FEATURE, "rb_raw")
        ra_raw = load_weight(nc, keep, W_rel[0:D, :], BY_FEATURE, "ra_raw")
        ga_raw = load_weight(nc, keep, W_gr[0:D, :], BY_FEATURE, "ga_raw")
        gb_raw = load_weight(nc, keep, W_gr[D : 2 * D, :], BY_FEATURE, "gb_raw")
        gc_raw = load_weight(nc, keep, W_gr[2 * D : 3 * D, :], BY_CHANNEL, "gc_raw")
        go_raw = load_weight(nc, keep, W_go, BY_FEATURE, "go_raw")

        brel_rows = keep.tile([P, P], BF16)
        nc.vector.memset(brel_rows[:], 0.0)
        bias_rows = keep.tile([P, 2, F], BF16)
        nc.vector.memset(bias_rows[:], 0.0)
        nc.scalar.dma_start(out=brel_rows[0:PACK, :], in_=b_rel.rearrange("(t m) -> t m", m=P))
        nc.scalar.dma_start(out=bias_rows[0:1, 0, :], in_=b_gr.rearrange("(o f) -> o f", o=1))
        nc.scalar.dma_start(out=bias_rows[0:1, 1, :], in_=b_go.rearrange("(o f) -> o f", o=1))

        warm = keep.tile([P, 1], F32)
        nc.vector.memset(warm[:], 0.0)
        nc.scalar.activation(out=warm[:], in_=warm[:], func=TANH)

        ident = keep.tile([P, P], F32)
        make_identity(nc, ident[:])
        ones = keep.tile([P, P], BF16)
        nc.vector.memset(ones[:], 1.0)

        x_codes = keep.tile([P, TOKENS], U32, align_bytes=64)
        x_scales = keep.tile([P, TOKENS], U8, align_bytes=64)
        x4_codes = keep.tile([P, TOKENS * BYTES_PER_WORD], U32, align_bytes=64)
        x4_scales = keep.tile([P, TOKENS * BYTES_PER_WORD], U8, align_bytes=64)
        nc.vector.memset(x_scales[:].bitcast(I32), 0)
        nc.vector.memset(x4_scales[:].bitcast(I32), 0)

        x_words = x_sb[:].bitcast(F32)
        x_t = setup_ps.tile([P, 2, TOKENS], F32, tag="setup")
        for u in range(2):
            nc.tensor.transpose(x_t[:, u, :], x_words[:, u : D // 2 : 2], ident[:])
        x_grouped = keep.tile([P, TOKENS, PACK], BF16, align_bytes=64)
        nc.scalar.copy(
            out=x_grouped[:].rearrange("p r t -> p (r t)").bitcast(F32).rearrange("p (r u) -> p r u", u=2),
            in_=x_t[:].rearrange("p u r -> p r u"),
        )
        x_fourfold = keep.tile([P, TOKENS, BYTES_PER_WORD, PACK], BF16, align_bytes=64)
        nc.vector.tensor_copy(
            out=x_fourfold[:],
            in_=x_grouped[:].unsqueeze(2).to_broadcast([P, TOKENS, BYTES_PER_WORD, PACK]),
        )
        nc.vector.quantize_mx(
            out=x_codes[:].bitcast(FP8X4), scales=x_scales[:], in_=x_grouped[:].rearrange("p r t -> p (r t)")
        )
        x_mx = (x_codes[:], x_scales[:])

        brel_rows_f32 = keep.tile([P, P], F32)
        nc.vector.tensor_copy(out=brel_rows_f32[:], in_=brel_rows[:])
        brel_t = setup_ps.tile([P, P], F32, tag="setup")
        nc.tensor.transpose(brel_t[:], brel_rows_f32[:], ident[:])
        bgr_ps = setup_ps.tile([P, F], F32, tag="setup")
        nc.tensor.matmul(out=bgr_ps[:], lhsT=ones[:], rhs=bias_rows[:, 0, :], start=True, stop=True)
        bgo_ps = setup_ps.tile([P, F], F32, tag="setup")
        nc.tensor.matmul(out=bgo_ps[:], lhsT=ones[:], rhs=bias_rows[:, 1, :], start=True, stop=True)

        rb_grouped = regroup_weight(keep, nc.scalar.copy, rb_raw, "rb_grouped")

        xj_codes = keep.tile([P, TOKENS * I_PER_TILE], U32, align_bytes=64)
        xj_scales = keep.tile([P, TOKENS * I_PER_TILE], U8, align_bytes=64)
        nc.vector.tensor_copy(
            out=xj_codes[:].bitcast(I32).rearrange("p (b c j) -> p b c j", b=BATCH, c=I_PER_TILE),
            in_=x_codes[:]
            .bitcast(I32)
            .rearrange("p (b j) -> p b j", b=BATCH)
            .unsqueeze(2)
            .to_broadcast([P, BATCH, I_PER_TILE, NODES]),
        )
        nc.vector.tensor_copy(
            out=xj_scales[:].bitcast(I32).rearrange("p (b c w) -> p b c w", b=BATCH, c=I_PER_TILE),
            in_=x_scales[:]
            .bitcast(I32)
            .rearrange("p (b w) -> p b w", b=BATCH)
            .unsqueeze(2)
            .to_broadcast([P, BATCH, I_PER_TILE, NODES // BYTES_PER_WORD]),
        )
        xj = (xj_codes, xj_scales)
        nc.vector.quantize_mx(
            out=x4_codes[:].bitcast(FP8X4),
            scales=x4_scales[:],
            in_=x_fourfold[:].rearrange("p r c t -> p (r c t)"),
        )
        brel = keep.tile([P, PACK], F32)
        nc.vector.tensor_copy(out=brel[:], in_=brel_t[:, 0:PACK])

        xi_codes = keep.tile([P, PAIRS], U32, align_bytes=64)
        xi_scales = keep.tile([P, PAIRS], U8, align_bytes=64)
        xi = (xi_codes, xi_scales)
        repeats = NODES // BYTES_PER_WORD

        def repeat_xi(b):
            tokens = slice(b * NODES, (b + 1) * NODES)
            nc.vector.tensor_copy(
                out=xi_codes[:]
                .bitcast(I32)
                .rearrange("p (r e c) -> p r e c", e=repeats, c=BYTES_PER_WORD)[:, tokens, :, :],
                in_=x4_codes[:]
                .bitcast(I32)
                .rearrange("p (r c) -> p r c", c=BYTES_PER_WORD)[:, tokens, :]
                .unsqueeze(2)
                .to_broadcast([P, NODES, repeats, BYTES_PER_WORD]),
            )
            nc.vector.tensor_copy(
                out=xi_scales[:].bitcast(I32).rearrange("p (r e) -> p r e", e=repeats)[:, tokens, :],
                in_=x4_scales[:].bitcast(I32)[:, tokens].unsqueeze(2).to_broadcast([P, NODES, repeats]),
            )

        ra_grouped = regroup_weight(keep, nc.vector.tensor_copy, ra_raw, "ra_grouped")
        rb = quantise_weight(nc, keep, rb_grouped, "rb")
        b_t = setup_ps.tile([P, PACK, TOKENS], F32, tag="setup")
        for t in range(PACK):
            mx_pass(nc, b_t[:, t, :], columns(rb, t * P, P), x_mx, start=True, stop=True)
        ra = quantise_weight(nc, keep, ra_grouped, "ra")
        a_t = keep_ps.tile([P, PACK, TOKENS], F32)
        for t in range(PACK):
            mx_pass(nc, a_t[:, t, :], columns(ra, t * P, P), x_mx, start=True, stop=True)
        repeat_xi(0)
        b_plus = keep.tile([P, TOKENS, PACK], F32)
        nc.vector.tensor_tensor(
            out=b_plus[:],
            in0=b_t[:].rearrange("p t r -> p r t"),
            in1=brel[:].unsqueeze(1).to_broadcast([P, TOKENS, PACK]),
            op=ADD,
        )
        a_sb = keep.tile([P, TOKENS, PACK], F32)
        nc.vector.tensor_copy(out=a_sb[:], in_=a_t[:].rearrange("p t r -> p r t"))
        ga_grouped = regroup_weight(keep, nc.scalar.copy, ga_raw, "ga_grouped")
        gb_grouped = regroup_weight(keep, nc.scalar.copy, gb_raw, "gb_grouped")
        gc_grouped = regroup_weight(keep, nc.scalar.copy, gc_raw, "gc_grouped")
        bgr = keep.tile([P, F], F32)
        nc.scalar.copy(out=bgr[:], in_=bgr_ps[:])
        go_grouped = regroup_weight(keep, nc.scalar.copy, go_raw, "go_grouped")
        bgo = keep.tile([P, F], F32)
        nc.scalar.copy(out=bgo[:], in_=bgo_ps[:])

        rel0_codes = keep.tile([P, PAIRS], U32, align_bytes=64)
        rel0_scales = keep.tile([P, PAIRS], U8, align_bytes=64)
        rel0_mx = (rel0_codes, rel0_scales)

        def form_rel0(chunk, gpsimd_i):
            first_token = chunk * I_PER_CHUNK
            b = first_token // NODES
            rel0 = stream.tile([P, I_PER_CHUNK, NODES, PACK], BF16, align_bytes=64)
            b_part = b_plus[:, b * NODES : (b + 1) * NODES, :].unsqueeze(1)
            nc.gpsimd.tensor_tensor(
                out=rel0[:, 0:gpsimd_i, :, :],
                in0=a_sb[:, first_token : first_token + gpsimd_i, :]
                .unsqueeze(2)
                .to_broadcast([P, gpsimd_i, NODES, PACK]),
                in1=b_part.to_broadcast([P, gpsimd_i, NODES, PACK]),
                op=ADD,
            )
            vector_i = I_PER_CHUNK - gpsimd_i
            nc.vector.tensor_tensor(
                out=rel0[:, gpsimd_i:I_PER_CHUNK, :, :],
                in0=a_t[:, :, first_token + gpsimd_i : first_token + I_PER_CHUNK]
                .rearrange("p t i -> p i t")
                .unsqueeze(2)
                .to_broadcast([P, vector_i, NODES, PACK]),
                in1=b_part.to_broadcast([P, vector_i, NODES, PACK]),
                op=ADD,
            )
            return rel0

        def quantise_rel0(chunk, rel0):
            chunk_codes, chunk_scales = columns(rel0_mx, chunk * COLS_PER_CHUNK, COLS_PER_CHUNK)
            nc.vector.quantize_mx(
                out=chunk_codes.bitcast(FP8X4), scales=chunk_scales, in_=rel0[:].rearrange("p i j t -> p (i j t)")
            )

        def open_tile(first_row):
            b = first_row // (NODES * NODES)
            acc = acc_ps.tile([P, F], F32)
            mx_pass(nc, acc[:], columns(xi, first_row, P), columns(ga, 0, F), start=True, stop=False)
            mx_pass(nc, acc[:], columns(xj, b * P, P), columns(gb, 0, F), start=False, stop=False)
            return acc

        def close_tile(acc, first_row):
            mx_pass(nc, acc[:], columns(rel0_mx, first_row, P), columns(gc, 0, F), start=False, stop=True)

        def finish(acc, bias, rows):
            result = results.tile([P, F], F32)
            nc.vector.tensor_tensor(out=result[:], in0=acc[:], in1=bias[:], op=ADD)
            nc.scalar.activation(out=result[:], in_=result[:], func=TANH)
            nc.sync.dma_start(out=rows, in_=result[:])

        def first_row_of(chunk, n):
            return chunk * COLS_PER_CHUNK + n * P

        def finish_rel(chunk, n, acc):
            finish(acc, bgr, rel_rows[first_row_of(chunk, n) : first_row_of(chunk, n) + P, :])

        rel0 = form_rel0(0, I_PER_CHUNK - GPSIMD_I)
        ga = quantise_weight(nc, keep, ga_grouped, "ga")
        gb = quantise_weight(nc, keep, gb_grouped, "gb")
        accs = [open_tile(first_row_of(0, n)) for n in range(TILES_PER_CHUNK)]
        gc = quantise_weight(nc, keep, gc_grouped, "gc")
        quantise_rel0(0, rel0)
        for n in range(TILES_PER_CHUNK):
            close_tile(accs[n], first_row_of(0, n))

        for chunk in range(1, CHUNKS):
            rel0 = form_rel0(chunk, GPSIMD_I)
            for n in range(TILES_PER_CHUNK):
                finish_rel(chunk - 1, n, accs[n])
                accs[n] = open_tile(first_row_of(chunk, n))
            if (chunk + 1) % CHUNKS_PER_BATCH == 0 and chunk + 1 < CHUNKS:
                repeat_xi((chunk + 1) // CHUNKS_PER_BATCH)
            quantise_rel0(chunk, rel0)
            for n in range(TILES_PER_CHUNK):
                close_tile(accs[n], first_row_of(chunk, n))

        go = quantise_weight(nc, keep, go_grouped, "go")
        new_x_acc = setup_ps.tile([P, F], F32, tag="setup")
        mx_pass(nc, new_x_acc[:], x_mx, columns(go, 0, F), start=True, stop=True)
        for n in range(TILES_PER_CHUNK):
            finish_rel(CHUNKS - 1, n, accs[n])
        finish(new_x_acc, bgo, new_x_rows)
